import numpy as np
import ml_dtypes


BF16 = ml_dtypes.bfloat16


def bf(x):
    return np.asarray(x, np.float32).astype(BF16)


def f64(x):
    return np.asarray(x).astype(np.float64)


E2M1 = np.array([0.0, 0.5, 1.0, 1.5, 2.0, 3.0, 4.0, 6.0, -0.0, -0.5, -1.0, -1.5, -2.0, -3.0, -4.0, -6.0])


def pack_weight(w, fmt):
    k, n = w.shape
    w = f64(bf(w)).reshape(k // 32, 32, n)
    amax = np.abs(w).max(1)
    if fmt == "e4m3":
        byte = np.frexp(amax)[1] - 1 + 127 - 7
    else:
        mant, ex = np.frexp(amax / 6.0)
        byte = np.where(mant > 0.5, ex, ex - 1) + 127
    byte = np.clip(np.where(amax > 0, byte, 1), 1, 254)
    scaled = (w * np.exp2(127.0 - byte)[:, None, :]).reshape(k, n).astype(np.float32)
    by_word = np.ascontiguousarray(scaled.reshape(k // 512, 128, 4, n).transpose(0, 1, 3, 2))
    if fmt == "e4m3":
        words = by_word.astype(ml_dtypes.float8_e4m3fn).view(np.uint8)
    else:
        c = by_word.astype(ml_dtypes.float4_e2m1fn).view(np.uint8) & 0xF
        words = c[..., 0::2] | (c[..., 1::2] << 4)
    return np.ascontiguousarray(words), np.ascontiguousarray(byte.astype(np.uint8).reshape(k // 512, 16, n))


def unpack_weight(words, scales, fmt):
    g, p, n, _ = words.shape
    if fmt == "e4m3":
        vals = np.ascontiguousarray(words).view(ml_dtypes.float8_e4m3fn).astype(np.float64)
    else:
        nib = np.empty((g, p, n, 4), np.uint8)
        nib[..., 0::2] = words & 0xF
        nib[..., 1::2] = words >> 4
        vals = E2M1[nib]
    vals = vals * np.repeat(np.exp2(scales.astype(np.float64) - 127.0), 8, axis=1)[..., None]
    return vals.transpose(0, 1, 3, 2).reshape(g * 512, n)

def pack4(w):
    words, scales = pack_weight(w, "e2m1")
    return words.reshape(words.shape[0], 128, -1), scales


def unpack4(words, scales):
    return unpack_weight(words.reshape(words.shape[0], 128, -1, 2), scales, "e2m1")


def kspread(k):
    return np.exp2(np.repeat(np.random.randint(-6, 7, k // 32), 32).astype(np.float64))


B, T, D, H, KV, HD, QB = 1, 2048, 2048, 8, 1, 128, 512
HALF = HD // 2
THETA = 100000.0


def rope_tables():
    inv_freq = 1.0 / THETA ** (np.arange(0, HD, 2) / HD)
    ang = np.arange(T)[:, None] * inv_freq[None, :]
    return np.cos(ang), np.sin(ang)


def apply_rope(a, cos, sin):
    ar = a.reshape(a.shape[:-1] + (HALF, 2))
    a0, a1 = ar[..., 0], ar[..., 1]
    c = cos[None, :, None, :]
    s = sin[None, :, None, :]
    o0 = a0 * c - a1 * s
    o1 = a0 * s + a1 * c
    return np.stack([o0, o1], axis=-1).reshape(a.shape)


def setup_inputs():
    s = kspread(D)
    cos, sin = rope_tables()
    x = np.random.standard_normal((B, T, D)) * s
    x_words, x_scales = pack4(x.reshape(B * T, D).T)
    Wq_words, Wq_scales = pack4(np.random.standard_normal((D, H * HD)) * 1.5 / np.sqrt(D) / s[:, None])
    Wk_words, Wk_scales = pack4(np.random.standard_normal((D, KV * HD)) * 1.5 / np.sqrt(D) / s[:, None])
    Wv_words, Wv_scales = pack4(np.random.standard_normal((D, KV * HD)) / np.sqrt(D) / s[:, None])
    return {"x_words": x_words, "x_scales": x_scales,
            "Wq_words": Wq_words, "Wq_scales": Wq_scales,
            "Wk_words": Wk_words, "Wk_scales": Wk_scales,
            "Wv_words": Wv_words, "Wv_scales": Wv_scales,
            "cos": bf(cos), "sin": bf(sin)}


def reference(x_words, x_scales, Wq_words, Wq_scales, Wk_words, Wk_scales, Wv_words, Wv_scales, cos, sin):
    xq = unpack4(x_words, x_scales).T.reshape(B, T, D)
    q = (xq @ unpack4(Wq_words, Wq_scales)).reshape(B, T, H, HD)
    k = (xq @ unpack4(Wk_words, Wk_scales)).reshape(B, T, KV, HD)
    v = (xq @ unpack4(Wv_words, Wv_scales)).reshape(B, T, KV, HD)
    q = apply_rope(q, f64(cos), f64(sin))
    k = apply_rope(k, f64(cos), f64(sin))
    return q, k[:, :, 0, :], v[:, :, 0, :]

@@ -1,0 +1,229 @@
+from contextlib import ExitStack
+
+import concourse.mybir as mybir
+
+T_TOK, D_IN, N_Q, HD = 2048, 2048, 1024, 128
+FLOPS = 2 * T_TOK * D_IN * (N_Q + 2 * HD)
+
+F32 = mybir.dt.float32
+BF16 = mybir.dt.bfloat16
+U8 = mybir.dt.uint8
+I32 = mybir.dt.int32
+FP4X4 = mybir.dt.float4_e2m1fn_x4
+ALU = mybir.AluOpType
+
+P = 128
+PASSES = 4
+TILES = T_TOK // P
+X_CHUNKS = [2, 4, 10]
+TABLE0 = 4
+BLOCK = 4
+VECTOR_TAIL = 2
+WARM = 12
+V_BANKS = [4, 4, 4, 3, 1]
+
+
+def tile_attention_pa_kernel(
+    tc, x_words, x_scales, Wq_words, Wq_scales, Wk_words, Wk_scales, Wv_words, Wv_scales, cos, sin, out_0, out_1, out_2
+):
+    nc = tc.nc
+    q_out = out_0.rearrange("b t h d -> (b t) (h d)")
+    k_out = out_1.rearrange("b (m p) d -> p (b m) d", p=P)
+    v_out = out_2.rearrange("b (m p) d -> p (b m) d", p=P)
+
+    with ExitStack() as ctx:
+        keep = ctx.enter_context(tc.tile_pool(name="keep", bufs=1))
+        prod = ctx.enter_context(tc.tile_pool(name="prod", bufs=8))
+        res = ctx.enter_context(tc.tile_pool(name="res", bufs=4))
+        kprod = ctx.enter_context(tc.tile_pool(name="kprod", bufs=2))
+        kres = ctx.enter_context(tc.tile_pool(name="kres", bufs=2))
+        vres = ctx.enter_context(tc.tile_pool(name="vres", bufs=3))
+        psum = ctx.enter_context(tc.psum_pool(name="psum", bufs=8))
+
+        x_codes = []
+        x_planes = []
+        x_first = []
+        where = {}
+        first = 0
+        for c, count in enumerate(X_CHUNKS):
+            xc_new = keep.tile([P, PASSES, 2 * P * count], U8, align_bytes=64, tag="xc%d" % c)
+            xs_new = keep.tile([P, PASSES, P * count], U8, align_bytes=64, tag="xs%d" % c)
+            x_codes.append(xc_new)
+            x_planes.append(xs_new)
+            x_first.append(first)
+            for j in range(count):
+                where[first + j] = (c, j)
+            first += count
+        wcq0 = keep.tile([P, PASSES, 1024], U8, align_bytes=64)
+        wcq1 = keep.tile([P, PASSES, 1024], U8, align_bytes=64)
+        wck = keep.tile([P, PASSES, 2 * HD], U8, align_bytes=64)
+        wcv = keep.tile([P, PASSES, 2 * HD], U8, align_bytes=64)
+        wsq0 = keep.tile([P, PASSES, 512], U8, align_bytes=64)
+        wsq1 = keep.tile([P, PASSES, 512], U8, align_bytes=64)
+        wsk = keep.tile([P, PASSES, HD], U8, align_bytes=64)
+        wsv = keep.tile([P, PASSES, HD], U8, align_bytes=64)
+        cos0 = keep.tile([P, TABLE0, HD // 2], BF16)
+        sin0 = keep.tile([P, TABLE0, HD // 2], BF16)
+        cos1 = keep.tile([P, TILES - TABLE0, HD // 2], BF16)
+        sin1 = keep.tile([P, TILES - TABLE0, HD // 2], BF16)
+        table = keep.tile([P, TILES, 2, HD], F32)
+        warm_in = keep.tile([P, 8], F32)
+        warm_out = keep.tile([P, 8], F32)
+        zeros = keep.tile([P, P + 512], BF16)
+
+        def load_codes(dst, src, c0, c1):
+            nc.sync.dma_start(out=dst[:].bitcast(I32), in_=src[:, :, c0:c1].rearrange("g p n -> p g n").bitcast(I32))
+
+        def load_scales(dst, src, c0, c1, quads):
+            for quad in quads:
+                nc.sync.dma_start(
+                    out=dst[32 * quad : 32 * quad + 4, :, :].bitcast(I32),
+                    in_=src[:, 4 * quad : 4 * quad + 4, c0:c1].rearrange("g r n -> r g n").bitcast(I32),
+                )
+
+        def load_x_scales(c, quads):
+            load_scales(x_planes[c], x_scales, P * x_first[c], P * (x_first[c] + X_CHUNKS[c]), quads)
+
+        def load_x_codes(c):
+            load_codes(x_codes[c], x_words, 2 * P * x_first[c], 2 * P * (x_first[c] + X_CHUNKS[c]))
+
+        for plane in (x_planes[0], wsq0, wsq1, x_planes[1], wsk, x_planes[2], wsv):
+            nc.vector.memset(plane[:].bitcast(I32), 0)
+        nc.gpsimd.memset(zeros[:], 0.0)
+        nc.gpsimd.memset(warm_in[:], 0.0)
+        nc.scalar.copy(out=warm_out[:], in_=warm_in[:])
+        cos_v = cos.rearrange("(m p) i -> p m i", p=P)
+        sin_v = sin.rearrange("(m p) i -> p m i", p=P)
+        nc.gpsimd.dma_start(out=cos0[:], in_=cos_v[:, 0:TABLE0, :])
+        nc.gpsimd.dma_start(out=sin0[:], in_=sin_v[:, 0:TABLE0, :])
+
+        every = [0, 1, 2, 3]
+        load_x_scales(0, every)
+        load_scales(wsq0, Wq_scales, 0, 512, [0, 1])
+        load_x_codes(0)
+        load_codes(wcq0, Wq_words, 0, 1024)
+        load_scales(wsq0, Wq_scales, 0, 512, [2, 3])
+        load_codes(wcq1, Wq_words, 1024, 2048)
+        load_scales(wsq1, Wq_scales, 512, 1024, every)
+        load_x_scales(1, every)
+        load_x_codes(1)
+        load_codes(wck, Wk_words, 0, 2 * HD)
+        load_scales(wsk, Wk_scales, 0, HD, every)
+        nc.sync.dma_start(out=cos1[:], in_=cos_v[:, TABLE0:TILES, :])
+        nc.sync.dma_start(out=sin1[:], in_=sin_v[:, TABLE0:TILES, :])
+        load_x_scales(2, every)
+        load_x_codes(2)
+        load_scales(wsv, Wv_scales, 0, HD, every)
+        load_codes(wcv, Wv_words, 0, 2 * HD)
+
+        if WARM:
+            dummy = psum.tile([P, 512], F32, tag="acc")
+            for i in range(WARM):
+                nc.tensor.matmul(out=dummy[:], lhsT=zeros[:, 0:P], rhs=zeros[:, P : P + 512], start=True, stop=True)
+
+        def build_table(m):
+            pairs = table[:, m, :, :].rearrange("p r (i e) -> p r i e", e=2)
+            cos_m = cos0[:, m, :] if m < TABLE0 else cos1[:, m - TABLE0, :]
+            sin_m = sin0[:, m, :] if m < TABLE0 else sin1[:, m - TABLE0, :]
+            nc.scalar.copy(out=pairs[:, 0, :, :], in_=cos_m.unsqueeze(2).to_broadcast([P, HD // 2, 2]))
+            nc.scalar.copy(out=pairs[:, 1, :, 0], in_=sin_m)
+            nc.scalar.mul(out=pairs[:, 1, :, 1], in_=sin_m, mul=-1.0)
+
+        def project(acc, m, wc, ws):
+            c, j = where[m]
+            for g in range(PASSES):
+                nc.tensor.matmul_mx(
+                    out=acc,
+                    lhsT=x_codes[c][:, g, 256 * j : 256 * (j + 1)].bitcast(FP4X4),
+                    lhsT_scale=x_planes[c][:, g, P * j : P * (j + 1)],
+                    rhs=wc[:, g, :].bitcast(FP4X4),
+                    rhs_scale=ws[:, g, :],
+                    start=(g == 0),
+                    stop=(g == PASSES - 1),
+                )
+
+        def swapped_add(adder, out, both):
+            adder.tensor_tensor(
+                out=out.rearrange("p (n e) -> p n e", e=2),
+                in0=both[:, 0, :].rearrange("p (n e) -> p n e", e=2),
+                in1=both[:, 1, :].rearrange("p (n e) -> p n e", e=2)[:, :, ::-1],
+                op=ALU.add,
+            )
+
+        def multiply(out, acc, tab):
+            nc.vector.tensor_tensor(
+                out=out.rearrange("p r (h d) -> p r h d", d=HD),
+                in0=acc.rearrange("p (h d) -> p h d", d=HD).unsqueeze(1).to_broadcast([P, 2, 4, HD]),
+                in1=tab,
+                op=ALU.mult,
+            )
+
+        products = {}
+
+        def q_half(m, half):
+            if m not in products:
+                t_new = prod.tile([P, 2, N_Q], F32, tag="products")
+                products[m] = t_new
+            acc = psum.tile([P, 512], F32, tag="acc")
+            project(acc[:], m, (wcq0, wcq1)[half], (wsq0, wsq1)[half])
+            multiply(
+                products[m][:, :, 512 * half : 512 * (half + 1)],
+                acc[:],
+                table[:, m, :, :].unsqueeze(2).to_broadcast([P, 2, 4, HD]),
+            )
+
+        def q_finish(m):
+            if m < TILES - VECTOR_TAIL:
+                o_m = res.tile([P, N_Q], F32, tag="results")
+                swapped_add(nc.gpsimd, o_m[:], products[m][:])
+                nc.sync.dma_start(out=q_out[P * m : P * (m + 1), :], in_=o_m[:])
+            if m + BLOCK < TILES:
+                build_table(m + BLOCK)
+
+        def k_block(b):
+            acc = psum.tile([P, 512], F32, tag="acc")
+            for i in range(BLOCK):
+                project(acc[:, HD * i : HD * (i + 1)], BLOCK * b + i, wck, wsk)
+            t_k = kprod.tile([P, 2, BLOCK * HD], F32, tag="kproducts")
+            multiply(t_k[:], acc[:], table[:, BLOCK * b : BLOCK * (b + 1), :, :].rearrange("p m r d -> p r m d"))
+            o_k = kres.tile([P, BLOCK * HD], F32, tag="kresults")
+            swapped_add(nc.gpsimd, o_k[:], t_k[:])
+            nc.sync.dma_start(
+                out=k_out[:, BLOCK * b : BLOCK * (b + 1), :], in_=o_k[:].rearrange("p (m d) -> p m d", d=HD)
+            )
+
+        for m in range(BLOCK):
+            build_table(m)
+
+        q_half(0, 0)
+        q_half(1, 0)
+        q_half(0, 1)
+        q_finish(0)
+        q_half(1, 1)
+        q_finish(1)
+        for m in (2, 3):
+            q_half(m, 0)
+            q_half(m, 1)
+            q_finish(m)
+        k_block(0)
+        for b in range(1, TILES // BLOCK):
+            k_block(b)
+            for m in range(BLOCK * b, BLOCK * (b + 1)):
+                q_half(m, 0)
+                q_half(m, 1)
+                q_finish(m)
+
+        for m in range(TILES - VECTOR_TAIL, TILES):
+            o_m = res.tile([P, N_Q], F32, tag="results")
+            swapped_add(nc.vector, o_m[:], products[m][:])
+            nc.sync.dma_start(out=q_out[P * m : P * (m + 1), :], in_=o_m[:])
+
+        m0 = 0
+        for count in V_BANKS:
+            acc = psum.tile([P, 512], F32, tag="acc")
+            for i in range(count):
+                project(acc[:, HD * i : HD * (i + 1)], m0 + i, wcv, wsv)
+            v_sb = vres.tile([P, 4, HD], F32, tag="v")
+            nc.scalar.copy(out=v_sb[:, 0:count, :], in_=acc[:, 0 : HD * count].rearrange("p (m d) -> p m d", d=HD))
+            nc.scalar.dma_start(out=v_out[:, m0 : m0 + count, :], in_=v_sb[:, 0:count, :])
+            m0 += count

@@ -18,9 +18,10 @@ TILES = T_TOK // P
 X_CHUNKS = [2, 4, 10]
 TABLE0 = 4
 BLOCK = 4
-VECTOR_TAIL = 2
+HALVED = (0, 1, 15)
+MERGED = 3
 WARM = 12
-V_BANKS = [4, 4, 4, 3, 1]
+V_BANKS = [3, 1]
 
 
 def tile_attention_pa_kernel(
@@ -56,12 +57,10 @@ def tile_attention_pa_kernel(
             first += count
         wcq0 = keep.tile([P, PASSES, 1024], U8, align_bytes=64)
         wcq1 = keep.tile([P, PASSES, 1024], U8, align_bytes=64)
-        wck = keep.tile([P, PASSES, 2 * HD], U8, align_bytes=64)
-        wcv = keep.tile([P, PASSES, 2 * HD], U8, align_bytes=64)
+        wckv = keep.tile([P, PASSES, 4 * HD], U8, align_bytes=64)
         wsq0 = keep.tile([P, PASSES, 512], U8, align_bytes=64)
         wsq1 = keep.tile([P, PASSES, 512], U8, align_bytes=64)
-        wsk = keep.tile([P, PASSES, HD], U8, align_bytes=64)
-        wsv = keep.tile([P, PASSES, HD], U8, align_bytes=64)
+        wskv = keep.tile([P, PASSES, 2 * HD], U8, align_bytes=64)
         cos0 = keep.tile([P, TABLE0, HD // 2], BF16)
         sin0 = keep.tile([P, TABLE0, HD // 2], BF16)
         cos1 = keep.tile([P, TILES - TABLE0, HD // 2], BF16)
@@ -72,12 +71,12 @@ def tile_attention_pa_kernel(
         zeros = keep.tile([P, P + 512], BF16)
 
         def load_codes(dst, src, c0, c1):
-            nc.sync.dma_start(out=dst[:].bitcast(I32), in_=src[:, :, c0:c1].rearrange("g p n -> p g n").bitcast(I32))
+            nc.sync.dma_start(out=dst.bitcast(I32), in_=src[:, :, c0:c1].rearrange("g p n -> p g n").bitcast(I32))
 
-        def load_scales(dst, src, c0, c1, quads):
+        def load_scales(dst, src, c0, c1, quads, d0=0):
             for quad in quads:
                 nc.sync.dma_start(
-                    out=dst[32 * quad : 32 * quad + 4, :, :].bitcast(I32),
+                    out=dst[32 * quad : 32 * quad + 4, :, d0 : d0 + c1 - c0].bitcast(I32),
                     in_=src[:, 4 * quad : 4 * quad + 4, c0:c1].rearrange("g r n -> r g n").bitcast(I32),
                 )
 
@@ -85,9 +84,9 @@ def tile_attention_pa_kernel(
             load_scales(x_planes[c], x_scales, P * x_first[c], P * (x_first[c] + X_CHUNKS[c]), quads)
 
         def load_x_codes(c):
-            load_codes(x_codes[c], x_words, 2 * P * x_first[c], 2 * P * (x_first[c] + X_CHUNKS[c]))
+            load_codes(x_codes[c][:], x_words, 2 * P * x_first[c], 2 * P * (x_first[c] + X_CHUNKS[c]))
 
-        for plane in (x_planes[0], wsq0, wsq1, x_planes[1], wsk, x_planes[2], wsv):
+        for plane in (x_planes[0], wsq0, wsq1, x_planes[1], wskv, x_planes[2]):
             nc.vector.memset(plane[:].bitcast(I32), 0)
         nc.gpsimd.memset(zeros[:], 0.0)
         nc.gpsimd.memset(warm_in[:], 0.0)
@@ -101,20 +100,21 @@ def tile_attention_pa_kernel(
         load_x_scales(0, every)
         load_scales(wsq0, Wq_scales, 0, 512, [0, 1])
         load_x_codes(0)
-        load_codes(wcq0, Wq_words, 0, 1024)
+        load_codes(wcq0[:], Wq_words, 0, 1024)
         load_scales(wsq0, Wq_scales, 0, 512, [2, 3])
-        load_codes(wcq1, Wq_words, 1024, 2048)
+        load_codes(wcq1[:], Wq_words, 1024, 2048)
         load_scales(wsq1, Wq_scales, 512, 1024, every)
         load_x_scales(1, every)
         load_x_codes(1)
-        load_codes(wck, Wk_words, 0, 2 * HD)
-        load_scales(wsk, Wk_scales, 0, HD, every)
+        load_codes(wckv[:, :, 0 : 2 * HD], Wk_words, 0, 2 * HD)
+        load_scales(wskv, Wk_scales, 0, HD, every)
         nc.sync.dma_start(out=cos1[:], in_=cos_v[:, TABLE0:TILES, :])
         nc.sync.dma_start(out=sin1[:], in_=sin_v[:, TABLE0:TILES, :])
-        load_x_scales(2, every)
+        load_x_scales(2, [0])
+        load_codes(wckv[:, :, 2 * HD : 4 * HD], Wv_words, 0, 2 * HD)
+        load_scales(wskv, Wv_scales, 0, HD, every, HD)
+        load_x_scales(2, [1, 2, 3])
         load_x_codes(2)
-        load_scales(wsv, Wv_scales, 0, HD, every)
-        load_codes(wcv, Wv_words, 0, 2 * HD)
 
         if WARM:
             dummy = psum.tile([P, 512], F32, tag="acc")
@@ -129,65 +129,100 @@ def tile_attention_pa_kernel(
             nc.scalar.copy(out=pairs[:, 1, :, 0], in_=sin_m)
             nc.scalar.mul(out=pairs[:, 1, :, 1], in_=sin_m, mul=-1.0)
 
-        def project(acc, m, wc, ws):
+        def project(acc, m, wc, ws, c0, c1):
             c, j = where[m]
             for g in range(PASSES):
                 nc.tensor.matmul_mx(
                     out=acc,
                     lhsT=x_codes[c][:, g, 256 * j : 256 * (j + 1)].bitcast(FP4X4),
                     lhsT_scale=x_planes[c][:, g, P * j : P * (j + 1)],
-                    rhs=wc[:, g, :].bitcast(FP4X4),
-                    rhs_scale=ws[:, g, :],
+                    rhs=wc[:, g, 2 * c0 : 2 * c1].bitcast(FP4X4),
+                    rhs_scale=ws[:, g, c0:c1],
                     start=(g == 0),
                     stop=(g == PASSES - 1),
                 )
 
-        def swapped_add(adder, out, both):
+        def swapped_add(adder, out, plain, crossed):
             adder.tensor_tensor(
-                out=out.rearrange("p (n e) -> p n e", e=2),
-                in0=both[:, 0, :].rearrange("p (n e) -> p n e", e=2),
-                in1=both[:, 1, :].rearrange("p (n e) -> p n e", e=2)[:, :, ::-1],
+                out=out.rearrange("p c (n e) -> p c n e", e=2),
+                in0=plain.rearrange("p c (n e) -> p c n e", e=2),
+                in1=crossed.rearrange("p c (n e) -> p c n e", e=2)[:, :, :, ::-1],
                 op=ALU.add,
             )
 
         def multiply(out, acc, tab):
             nc.vector.tensor_tensor(
                 out=out.rearrange("p r (h d) -> p r h d", d=HD),
-                in0=acc.rearrange("p (h d) -> p h d", d=HD).unsqueeze(1).to_broadcast([P, 2, 4, HD]),
+                in0=acc.unsqueeze(1).to_broadcast([P, 2, acc.shape[1], HD]),
                 in1=tab,
                 op=ALU.mult,
             )
 
         products = {}
+        results = {}
 
         def q_half(m, half):
             if m not in products:
-                t_new = prod.tile([P, 2, N_Q], F32, tag="products")
+                t_new = prod.tile([P, 2, 2, 512], F32, tag="products")
                 products[m] = t_new
+                o_new = res.tile([P, 2, 512], F32, tag="results")
+                results[m] = o_new
             acc = psum.tile([P, 512], F32, tag="acc")
-            project(acc[:], m, (wcq0, wcq1)[half], (wsq0, wsq1)[half])
+            project(acc[:], m, (wcq0, wcq1)[half], (wsq0, wsq1)[half], 0, 512)
             multiply(
-                products[m][:, :, 512 * half : 512 * (half + 1)],
-                acc[:],
+                products[m][:, half, :, :],
+                acc[:].rearrange("p (h d) -> p h d", d=HD),
                 table[:, m, :, :].unsqueeze(2).to_broadcast([P, 2, 4, HD]),
             )
+            if m in HALVED:
+                adder = nc.vector if m == TILES - 1 else nc.gpsimd
+                swapped_add(
+                    adder,
+                    results[m][:, half : half + 1, :],
+                    products[m][:, half : half + 1, 0, :],
+                    products[m][:, half : half + 1, 1, :],
+                )
+                if m == TILES - 1:
+                    nc.sync.dma_start(
+                        out=q_out[P * m : P * (m + 1), 512 * half : 512 * (half + 1)], in_=results[m][:, half, :]
+                    )
 
         def q_finish(m):
-            if m < TILES - VECTOR_TAIL:
-                o_m = res.tile([P, N_Q], F32, tag="results")
-                swapped_add(nc.gpsimd, o_m[:], products[m][:])
-                nc.sync.dma_start(out=q_out[P * m : P * (m + 1), :], in_=o_m[:])
+            if m not in HALVED:
+                swapped_add(nc.gpsimd, results[m][:], products[m][:, :, 0, :], products[m][:, :, 1, :])
+            if m < TILES - 1:
+                nc.sync.dma_start(out=q_out[P * m : P * (m + 1), :], in_=results[m][:].rearrange("p c n -> p (c n)"))
             if m + BLOCK < TILES:
                 build_table(m + BLOCK)
 
         def k_block(b):
-            acc = psum.tile([P, 512], F32, tag="acc")
-            for i in range(BLOCK):
-                project(acc[:, HD * i : HD * (i + 1)], BLOCK * b + i, wck, wsk)
             t_k = kprod.tile([P, 2, BLOCK * HD], F32, tag="kproducts")
-            multiply(t_k[:], acc[:], table[:, BLOCK * b : BLOCK * (b + 1), :, :].rearrange("p m r d -> p r m d"))
+            if b < MERGED:
+                v_sb = vres.tile([P, 4, HD], F32, tag="v")
+                for pair in range(BLOCK // 2):
+                    m0 = BLOCK * b + 2 * pair
+                    acc = psum.tile([P, 512], F32, tag="acc")
+                    for i in range(2):
+                        project(acc[:, 2 * HD * i : 2 * HD * (i + 1)], m0 + i, wckv, wskv, 0, 2 * HD)
+                    halves = acc[:].rearrange("p (m s d) -> p m s d", s=2, d=HD)
+                    multiply(
+                        t_k[:, :, 2 * HD * pair : 2 * HD * (pair + 1)],
+                        halves[:, :, 0, :],
+                        table[:, m0 : m0 + 2, :, :].rearrange("p m r d -> p r m d"),
+                    )
+                    nc.scalar.copy(out=v_sb[:, 2 * pair : 2 * pair + 2, :], in_=halves[:, :, 1, :])
+                nc.scalar.dma_start(out=v_out[:, BLOCK * b : BLOCK * (b + 1), :], in_=v_sb[:])
+            else:
+                acc = psum.tile([P, 512], F32, tag="acc")
+                for i in range(BLOCK):
+                    project(acc[:, HD * i : HD * (i + 1)], BLOCK * b + i, wckv, wskv, 0, HD)
+                multiply(
+                    t_k[:],
+                    acc[:].rearrange("p (m d) -> p m d", d=HD),
+                    table[:, BLOCK * b : BLOCK * (b + 1), :, :].rearrange("p m r d -> p r m d"),
+                )
             o_k = kres.tile([P, BLOCK * HD], F32, tag="kresults")
-            swapped_add(nc.gpsimd, o_k[:], t_k[:])
+            swapped_add(nc.gpsimd, o_k[:].unsqueeze(1), t_k[:, 0:1, :], t_k[:, 1:2, :])
             nc.sync.dma_start(
                 out=k_out[:, BLOCK * b : BLOCK * (b + 1), :], in_=o_k[:].rearrange("p (m d) -> p m d", d=HD)
             )
@@ -213,16 +248,11 @@ def tile_attention_pa_kernel(
                 q_half(m, 1)
                 q_finish(m)
 
-        for m in range(TILES - VECTOR_TAIL, TILES):
-            o_m = res.tile([P, N_Q], F32, tag="results")
-            swapped_add(nc.vector, o_m[:], products[m][:])
-            nc.sync.dma_start(out=q_out[P * m : P * (m + 1), :], in_=o_m[:])
-
-        m0 = 0
+        m0 = BLOCK * MERGED
         for count in V_BANKS:
             acc = psum.tile([P, 512], F32, tag="acc")
             for i in range(count):
-                project(acc[:, HD * i : HD * (i + 1)], m0 + i, wcv, wsv)
+                project(acc[:, HD * i : HD * (i + 1)], m0 + i, wckv, wskv, HD, 2 * HD)
             v_sb = vres.tile([P, 4, HD], F32, tag="v")
             nc.scalar.copy(out=v_sb[:, 0:count, :], in_=acc[:, 0 : HD * count].rearrange("p (m d) -> p m d", d=HD))
             nc.scalar.dma_start(out=v_out[:, m0 : m0 + count, :], in_=v_sb[:, 0:count, :])

@@ -18,7 +18,8 @@ TILES = T_TOK // P
 X_CHUNKS = [2, 4, 10]
 TABLE0 = 4
 BLOCK = 4
-HALVED = (0, 1, 15)
+HALVED = (0, 1, 14, 15)
+VECTOR_HALVES = ((14, 1), (15, 0), (15, 1))
 MERGED = 3
 WARM = 12
 V_BANKS = [3, 1]
@@ -174,23 +175,25 @@ def tile_attention_pa_kernel(
                 acc[:].rearrange("p (h d) -> p h d", d=HD),
                 table[:, m, :, :].unsqueeze(2).to_broadcast([P, 2, 4, HD]),
             )
-            if m in HALVED:
-                adder = nc.vector if m == TILES - 1 else nc.gpsimd
-                swapped_add(
-                    adder,
-                    results[m][:, half : half + 1, :],
-                    products[m][:, half : half + 1, 0, :],
-                    products[m][:, half : half + 1, 1, :],
+            if m in HALVED and (m, half) not in VECTOR_HALVES:
+                add_half(nc.gpsimd, m, half)
+
+        def add_half(adder, m, half):
+            swapped_add(
+                adder,
+                results[m][:, half : half + 1, :],
+                products[m][:, half : half + 1, 0, :],
+                products[m][:, half : half + 1, 1, :],
+            )
+            if m >= TILES - 2:
+                nc.sync.dma_start(
+                    out=q_out[P * m : P * (m + 1), 512 * half : 512 * (half + 1)], in_=results[m][:, half, :]
                 )
-                if m == TILES - 1:
-                    nc.sync.dma_start(
-                        out=q_out[P * m : P * (m + 1), 512 * half : 512 * (half + 1)], in_=results[m][:, half, :]
-                    )
 
         def q_finish(m):
             if m not in HALVED:
                 swapped_add(nc.gpsimd, results[m][:], products[m][:, :, 0, :], products[m][:, :, 1, :])
-            if m < TILES - 1:
+            if m < TILES - 2:
                 nc.sync.dma_start(out=q_out[P * m : P * (m + 1), :], in_=results[m][:].rearrange("p c n -> p (c n)"))
             if m + BLOCK < TILES:
                 build_table(m + BLOCK)
@@ -242,11 +245,16 @@ def tile_attention_pa_kernel(
             q_finish(m)
         k_block(0)
         for b in range(1, TILES // BLOCK):
-            k_block(b)
+            if b == MERGED:
+                k_block(b)
             for m in range(BLOCK * b, BLOCK * (b + 1)):
                 q_half(m, 0)
                 q_half(m, 1)
                 q_finish(m)
+            if b < MERGED:
+                k_block(b)
+        for m, half in VECTOR_HALVES:
+            add_half(nc.vector, m, half)
 
         m0 = BLOCK * MERGED
         for count in V_BANKS:

@@ -98,11 +98,11 @@ def tile_attention_pa_kernel(
         nc.gpsimd.dma_start(out=sin0[:], in_=sin_v[:, 0:TABLE0, :])
 
         every = [0, 1, 2, 3]
-        load_x_scales(0, every)
-        load_scales(wsq0, Wq_scales, 0, 512, [0, 1])
         load_x_codes(0)
+        load_x_scales(0, [0])
         load_codes(wcq0[:], Wq_words, 0, 1024)
-        load_scales(wsq0, Wq_scales, 0, 512, [2, 3])
+        load_x_scales(0, [1, 2, 3])
+        load_scales(wsq0, Wq_scales, 0, 512, every)
         load_codes(wcq1[:], Wq_words, 1024, 2048)
         load_scales(wsq1, Wq_scales, 512, 1024, every)
         load_x_scales(1, every)

@@ -87,15 +87,17 @@ def tile_attention_pa_kernel(
         def load_x_codes(c):
             load_codes(x_codes[c][:], x_words, 2 * P * x_first[c], 2 * P * (x_first[c] + X_CHUNKS[c]))
 
-        for plane in (x_planes[0], wsq0, wsq1, x_planes[1], wskv, x_planes[2]):
-            nc.vector.memset(plane[:].bitcast(I32), 0)
-        nc.gpsimd.memset(zeros[:], 0.0)
-        nc.gpsimd.memset(warm_in[:], 0.0)
-        nc.scalar.copy(out=warm_out[:], in_=warm_in[:])
         cos_v = cos.rearrange("(m p) i -> p m i", p=P)
         sin_v = sin.rearrange("(m p) i -> p m i", p=P)
-        nc.gpsimd.dma_start(out=cos0[:], in_=cos_v[:, 0:TABLE0, :])
-        nc.gpsimd.dma_start(out=sin0[:], in_=sin_v[:, 0:TABLE0, :])
+        nc.scalar.dma_start(out=cos0[:], in_=cos_v[:, 0:TABLE0, :])
+        nc.scalar.dma_start(out=sin0[:], in_=sin_v[:, 0:TABLE0, :])
+        for plane in (x_planes[0], wsq0):
+            nc.vector.memset(plane[:].bitcast(I32), 0)
+        nc.vector.memset(zeros[:], 0.0)
+        nc.vector.memset(warm_in[:], 0.0)
+        for plane in (wsq1, x_planes[1], wskv, x_planes[2]):
+            nc.vector.memset(plane[:].bitcast(I32), 0)
+        nc.scalar.copy(out=warm_out[:], in_=warm_in[:])
 
         every = [0, 1, 2, 3]
         load_x_codes(0)

@@ -89,8 +89,6 @@ def tile_attention_pa_kernel(
 
         cos_v = cos.rearrange("(m p) i -> p m i", p=P)
         sin_v = sin.rearrange("(m p) i -> p m i", p=P)
-        nc.scalar.dma_start(out=cos0[:], in_=cos_v[:, 0:TABLE0, :])
-        nc.scalar.dma_start(out=sin0[:], in_=sin_v[:, 0:TABLE0, :])
         for plane in (x_planes[0], wsq0):
             nc.vector.memset(plane[:].bitcast(I32), 0)
         nc.vector.memset(zeros[:], 0.0)
@@ -105,6 +103,8 @@ def tile_attention_pa_kernel(
         load_codes(wcq0[:], Wq_words, 0, 1024)
         load_x_scales(0, [1, 2, 3])
         load_scales(wsq0, Wq_scales, 0, 512, every)
+        nc.sync.dma_start(out=cos0[:], in_=cos_v[:, 0:TABLE0, :])
+        nc.sync.dma_start(out=sin0[:], in_=sin_v[:, 0:TABLE0, :])
         load_codes(wcq1[:], Wq_words, 1024, 2048)
         load_scales(wsq1, Wq_scales, 512, 1024, every)
         load_x_scales(1, every)

@@ -21,6 +21,7 @@ BLOCK = 4
 HALVED = (0, 1, 14, 15)
 VECTOR_HALVES = ((14, 1), (15, 0), (15, 1))
 MERGED = 3
+SHIFT = 128
 WARM = 12
 V_BANKS = [3, 1]
 
@@ -56,11 +57,13 @@ def tile_attention_pa_kernel(
             for j in range(count):
                 where[first + j] = (c, j)
             first += count
-        wcq0 = keep.tile([P, PASSES, 1024], U8, align_bytes=64)
-        wcq1 = keep.tile([P, PASSES, 1024], U8, align_bytes=64)
+        wcq0 = keep.tile([P, PASSES, 1024], U8, align_bytes=256)
+        wcq1 = keep.tile([P, PASSES, 1024], U8, align_bytes=256)
         wckv = keep.tile([P, PASSES, 4 * HD], U8, align_bytes=64)
-        wsq0 = keep.tile([P, PASSES, 512], U8, align_bytes=64)
-        wsq1 = keep.tile([P, PASSES, 512], U8, align_bytes=64)
+        wsq0_wide = keep.tile([P, SHIFT + PASSES * 512], U8, align_bytes=256)
+        wsq1_wide = keep.tile([P, SHIFT + PASSES * 512], U8, align_bytes=256)
+        wsq0 = wsq0_wide[:, SHIFT:].rearrange("p (g n) -> p g n", g=PASSES)
+        wsq1 = wsq1_wide[:, SHIFT:].rearrange("p (g n) -> p g n", g=PASSES)
         wskv = keep.tile([P, PASSES, 2 * HD], U8, align_bytes=64)
         cos0 = keep.tile([P, TABLE0, HD // 2], BF16)
         sin0 = keep.tile([P, TABLE0, HD // 2], BF16)
@@ -89,11 +92,11 @@ def tile_attention_pa_kernel(
 
         cos_v = cos.rearrange("(m p) i -> p m i", p=P)
         sin_v = sin.rearrange("(m p) i -> p m i", p=P)
-        for plane in (x_planes[0], wsq0):
+        for plane in (x_planes[0], wsq0_wide):
             nc.vector.memset(plane[:].bitcast(I32), 0)
         nc.vector.memset(zeros[:], 0.0)
         nc.vector.memset(warm_in[:], 0.0)
-        for plane in (wsq1, x_planes[1], wskv, x_planes[2]):
+        for plane in (wsq1_wide, x_planes[1], wskv, x_planes[2]):
             nc.vector.memset(plane[:].bitcast(I32), 0)
         nc.scalar.copy(out=warm_out[:], in_=warm_in[:])
 

@@ -78,10 +78,10 @@ def tile_attention_pa_kernel(
             nc.sync.dma_start(out=dst.bitcast(I32), in_=src[:, :, c0:c1].rearrange("g p n -> p g n").bitcast(I32))
 
         def load_scales(dst, src, c0, c1, quads, d0=0):
-            for quad in quads:
+            for row in quads:
                 nc.sync.dma_start(
-                    out=dst[32 * quad : 32 * quad + 4, :, d0 : d0 + c1 - c0].bitcast(I32),
-                    in_=src[:, 4 * quad : 4 * quad + 4, c0:c1].rearrange("g r n -> r g n").bitcast(I32),
+                    out=dst[row:P:32, :, d0 : d0 + c1 - c0].bitcast(I32),
+                    in_=src[:, row:16:4, c0:c1].rearrange("g q n -> q g n").bitcast(I32),
                 )
 
         def load_x_scales(c, quads):

from contextlib import ExitStack

import concourse.mybir as mybir

T_TOK, D_IN, N_Q, HD = 2048, 2048, 1024, 128
FLOPS = 2 * T_TOK * D_IN * (N_Q + 2 * HD)

F32 = mybir.dt.float32
BF16 = mybir.dt.bfloat16
U8 = mybir.dt.uint8
I32 = mybir.dt.int32
FP4X4 = mybir.dt.float4_e2m1fn_x4
ALU = mybir.AluOpType

P = 128
PASSES = 4
TILES = T_TOK // P
X_CHUNKS = [2, 4, 10]
TABLE0 = 4
BLOCK = 4
HALVED = (0, 1, 14, 15)
VECTOR_HALVES = ((14, 1), (15, 0), (15, 1))
MERGED = 3
SHIFT = 128
WARM = 12
V_BANKS = [3, 1]


def tile_attention_pa_kernel(
    tc, x_words, x_scales, Wq_words, Wq_scales, Wk_words, Wk_scales, Wv_words, Wv_scales, cos, sin, out_0, out_1, out_2
):
    nc = tc.nc
    q_out = out_0.rearrange("b t h d -> (b t) (h d)")
    k_out = out_1.rearrange("b (m p) d -> p (b m) d", p=P)
    v_out = out_2.rearrange("b (m p) d -> p (b m) d", p=P)

    with ExitStack() as ctx:
        keep = ctx.enter_context(tc.tile_pool(name="keep", bufs=1))
        prod = ctx.enter_context(tc.tile_pool(name="prod", bufs=8))
        res = ctx.enter_context(tc.tile_pool(name="res", bufs=4))
        kprod = ctx.enter_context(tc.tile_pool(name="kprod", bufs=2))
        kres = ctx.enter_context(tc.tile_pool(name="kres", bufs=2))
        vres = ctx.enter_context(tc.tile_pool(name="vres", bufs=3))
        psum = ctx.enter_context(tc.psum_pool(name="psum", bufs=8))

        x_codes = []
        x_planes = []
        x_first = []
        where = {}
        first = 0
        for c, count in enumerate(X_CHUNKS):
            xc_new = keep.tile([P, PASSES, 2 * P * count], U8, align_bytes=64, tag="xc%d" % c)
            xs_new = keep.tile([P, PASSES, P * count], U8, align_bytes=64, tag="xs%d" % c)
            x_codes.append(xc_new)
            x_planes.append(xs_new)
            x_first.append(first)
            for j in range(count):
                where[first + j] = (c, j)
            first += count
        wcq0 = keep.tile([P, PASSES, 1024], U8, align_bytes=256)
        wcq1 = keep.tile([P, PASSES, 1024], U8, align_bytes=256)
        wckv = keep.tile([P, PASSES, 4 * HD], U8, align_bytes=64)
        wsq0_wide = keep.tile([P, SHIFT + PASSES * 512], U8, align_bytes=256)
        wsq1_wide = keep.tile([P, SHIFT + PASSES * 512], U8, align_bytes=256)
        wsq0 = wsq0_wide[:, SHIFT:].rearrange("p (g n) -> p g n", g=PASSES)
        wsq1 = wsq1_wide[:, SHIFT:].rearrange("p (g n) -> p g n", g=PASSES)
        wskv = keep.tile([P, PASSES, 2 * HD], U8, align_bytes=64)
        cos0 = keep.tile([P, TABLE0, HD // 2], BF16)
        sin0 = keep.tile([P, TABLE0, HD // 2], BF16)
        cos1 = keep.tile([P, TILES - TABLE0, HD // 2], BF16)
        sin1 = keep.tile([P, TILES - TABLE0, HD // 2], BF16)
        table = keep.tile([P, TILES, 2, HD], F32)
        warm_in = keep.tile([P, 8], F32)
        warm_out = keep.tile([P, 8], F32)
        zeros = keep.tile([P, P + 512], BF16)

        def load_codes(dst, src, c0, c1):
            nc.sync.dma_start(out=dst.bitcast(I32), in_=src[:, :, c0:c1].rearrange("g p n -> p g n").bitcast(I32))

        def load_scales(dst, src, c0, c1, quads, d0=0):
            for row in quads:
                nc.sync.dma_start(
                    out=dst[row:P:32, :, d0 : d0 + c1 - c0].bitcast(I32),
                    in_=src[:, row:16:4, c0:c1].rearrange("g q n -> q g n").bitcast(I32),
                )

        def load_x_scales(c, quads):
            load_scales(x_planes[c], x_scales, P * x_first[c], P * (x_first[c] + X_CHUNKS[c]), quads)

        def load_x_codes(c):
            load_codes(x_codes[c][:], x_words, 2 * P * x_first[c], 2 * P * (x_first[c] + X_CHUNKS[c]))

        cos_v = cos.rearrange("(m p) i -> p m i", p=P)
        sin_v = sin.rearrange("(m p) i -> p m i", p=P)
        for plane in (x_planes[0], wsq0_wide):
            nc.vector.memset(plane[:].bitcast(I32), 0)
        nc.vector.memset(zeros[:], 0.0)
        nc.vector.memset(warm_in[:], 0.0)
        for plane in (wsq1_wide, x_planes[1], wskv, x_planes[2]):
            nc.vector.memset(plane[:].bitcast(I32), 0)
        nc.scalar.copy(out=warm_out[:], in_=warm_in[:])

        every = [0, 1, 2, 3]
        load_x_codes(0)
        load_x_scales(0, [0])
        load_codes(wcq0[:], Wq_words, 0, 1024)
        load_x_scales(0, [1, 2, 3])
        load_scales(wsq0, Wq_scales, 0, 512, every)
        nc.sync.dma_start(out=cos0[:], in_=cos_v[:, 0:TABLE0, :])
        nc.sync.dma_start(out=sin0[:], in_=sin_v[:, 0:TABLE0, :])
        load_codes(wcq1[:], Wq_words, 1024, 2048)
        load_scales(wsq1, Wq_scales, 512, 1024, every)
        load_x_scales(1, every)
        load_x_codes(1)
        load_codes(wckv[:, :, 0 : 2 * HD], Wk_words, 0, 2 * HD)
        load_scales(wskv, Wk_scales, 0, HD, every)
        nc.sync.dma_start(out=cos1[:], in_=cos_v[:, TABLE0:TILES, :])
        nc.sync.dma_start(out=sin1[:], in_=sin_v[:, TABLE0:TILES, :])
        load_x_scales(2, [0])
        load_codes(wckv[:, :, 2 * HD : 4 * HD], Wv_words, 0, 2 * HD)
        load_scales(wskv, Wv_scales, 0, HD, every, HD)
        load_x_scales(2, [1, 2, 3])
        load_x_codes(2)

        if WARM:
            dummy = psum.tile([P, 512], F32, tag="acc")
            for i in range(WARM):
                nc.tensor.matmul(out=dummy[:], lhsT=zeros[:, 0:P], rhs=zeros[:, P : P + 512], start=True, stop=True)

        def build_table(m):
            pairs = table[:, m, :, :].rearrange("p r (i e) -> p r i e", e=2)
            cos_m = cos0[:, m, :] if m < TABLE0 else cos1[:, m - TABLE0, :]
            sin_m = sin0[:, m, :] if m < TABLE0 else sin1[:, m - TABLE0, :]
            nc.scalar.copy(out=pairs[:, 0, :, :], in_=cos_m.unsqueeze(2).to_broadcast([P, HD // 2, 2]))
            nc.scalar.copy(out=pairs[:, 1, :, 0], in_=sin_m)
            nc.scalar.mul(out=pairs[:, 1, :, 1], in_=sin_m, mul=-1.0)

        def project(acc, m, wc, ws, c0, c1):
            c, j = where[m]
            for g in range(PASSES):
                nc.tensor.matmul_mx(
                    out=acc,
                    lhsT=x_codes[c][:, g, 256 * j : 256 * (j + 1)].bitcast(FP4X4),
                    lhsT_scale=x_planes[c][:, g, P * j : P * (j + 1)],
                    rhs=wc[:, g, 2 * c0 : 2 * c1].bitcast(FP4X4),
                    rhs_scale=ws[:, g, c0:c1],
                    start=(g == 0),
                    stop=(g == PASSES - 1),
                )

        def swapped_add(adder, out, plain, crossed):
            adder.tensor_tensor(
                out=out.rearrange("p c (n e) -> p c n e", e=2),
                in0=plain.rearrange("p c (n e) -> p c n e", e=2),
                in1=crossed.rearrange("p c (n e) -> p c n e", e=2)[:, :, :, ::-1],
                op=ALU.add,
            )

        def multiply(out, acc, tab):
            nc.vector.tensor_tensor(
                out=out.rearrange("p r (h d) -> p r h d", d=HD),
                in0=acc.unsqueeze(1).to_broadcast([P, 2, acc.shape[1], HD]),
                in1=tab,
                op=ALU.mult,
            )

        products = {}
        results = {}

        def q_half(m, half):
            if m not in products:
                t_new = prod.tile([P, 2, 2, 512], F32, tag="products")
                products[m] = t_new
                o_new = res.tile([P, 2, 512], F32, tag="results")
                results[m] = o_new
            acc = psum.tile([P, 512], F32, tag="acc")
            project(acc[:], m, (wcq0, wcq1)[half], (wsq0, wsq1)[half], 0, 512)
            multiply(
                products[m][:, half, :, :],
                acc[:].rearrange("p (h d) -> p h d", d=HD),
                table[:, m, :, :].unsqueeze(2).to_broadcast([P, 2, 4, HD]),
            )
            if m in HALVED and (m, half) not in VECTOR_HALVES:
                add_half(nc.gpsimd, m, half)

        def add_half(adder, m, half):
            swapped_add(
                adder,
                results[m][:, half : half + 1, :],
                products[m][:, half : half + 1, 0, :],
                products[m][:, half : half + 1, 1, :],
            )
            if m >= TILES - 2:
                nc.sync.dma_start(
                    out=q_out[P * m : P * (m + 1), 512 * half : 512 * (half + 1)], in_=results[m][:, half, :]
                )

        def q_finish(m):
            if m not in HALVED:
                swapped_add(nc.gpsimd, results[m][:], products[m][:, :, 0, :], products[m][:, :, 1, :])
            if m < TILES - 2:
                nc.sync.dma_start(out=q_out[P * m : P * (m + 1), :], in_=results[m][:].rearrange("p c n -> p (c n)"))
            if m + BLOCK < TILES:
                build_table(m + BLOCK)

        def k_block(b):
            t_k = kprod.tile([P, 2, BLOCK * HD], F32, tag="kproducts")
            if b < MERGED:
                v_sb = vres.tile([P, 4, HD], F32, tag="v")
                for pair in range(BLOCK // 2):
                    m0 = BLOCK * b + 2 * pair
                    acc = psum.tile([P, 512], F32, tag="acc")
                    for i in range(2):
                        project(acc[:, 2 * HD * i : 2 * HD * (i + 1)], m0 + i, wckv, wskv, 0, 2 * HD)
                    halves = acc[:].rearrange("p (m s d) -> p m s d", s=2, d=HD)
                    multiply(
                        t_k[:, :, 2 * HD * pair : 2 * HD * (pair + 1)],
                        halves[:, :, 0, :],
                        table[:, m0 : m0 + 2, :, :].rearrange("p m r d -> p r m d"),
                    )
                    nc.scalar.copy(out=v_sb[:, 2 * pair : 2 * pair + 2, :], in_=halves[:, :, 1, :])
                nc.scalar.dma_start(out=v_out[:, BLOCK * b : BLOCK * (b + 1), :], in_=v_sb[:])
            else:
                acc = psum.tile([P, 512], F32, tag="acc")
                for i in range(BLOCK):
                    project(acc[:, HD * i : HD * (i + 1)], BLOCK * b + i, wckv, wskv, 0, HD)
                multiply(
                    t_k[:],
                    acc[:].rearrange("p (m d) -> p m d", d=HD),
                    table[:, BLOCK * b : BLOCK * (b + 1), :, :].rearrange("p m r d -> p r m d"),
                )
            o_k = kres.tile([P, BLOCK * HD], F32, tag="kresults")
            swapped_add(nc.gpsimd, o_k[:].unsqueeze(1), t_k[:, 0:1, :], t_k[:, 1:2, :])
            nc.sync.dma_start(
                out=k_out[:, BLOCK * b : BLOCK * (b + 1), :], in_=o_k[:].rearrange("p (m d) -> p m d", d=HD)
            )

        for m in range(BLOCK):
            build_table(m)

        q_half(0, 0)
        q_half(1, 0)
        q_half(0, 1)
        q_finish(0)
        q_half(1, 1)
        q_finish(1)
        for m in (2, 3):
            q_half(m, 0)
            q_half(m, 1)
            q_finish(m)
        k_block(0)
        for b in range(1, TILES // BLOCK):
            if b == MERGED:
                k_block(b)
            for m in range(BLOCK * b, BLOCK * (b + 1)):
                q_half(m, 0)
                q_half(m, 1)
                q_finish(m)
            if b < MERGED:
                k_block(b)
        for m, half in VECTOR_HALVES:
            add_half(nc.vector, m, half)

        m0 = BLOCK * MERGED
        for count in V_BANKS:
            acc = psum.tile([P, 512], F32, tag="acc")
            for i in range(count):
                project(acc[:, HD * i : HD * (i + 1)], m0 + i, wckv, wskv, HD, 2 * HD)
            v_sb = vres.tile([P, 4, HD], F32, tag="v")
            nc.scalar.copy(out=v_sb[:, 0:count, :], in_=acc[:, 0 : HD * count].rearrange("p (m d) -> p m d", d=HD))
            nc.scalar.dma_start(out=v_out[:, m0 : m0 + count, :], in_=v_sb[:, 0:count, :])
            m0 += count
